import numpy as np
import ml_dtypes

BF16 = ml_dtypes.bfloat16


def bf(x):
    return np.asarray(x, np.float32).astype(BF16)


def f32(x):
    return np.asarray(x, np.float32)


def f64(x):
    return np.asarray(x).astype(np.float64)


def striped(idx):
    return np.tile(idx.reshape(-1, 16).T, (8, 1))


C, S, N = 512, 256, 128
RATE_HEAD = 0.88


def setup_inputs():
    return {"word_feat": f32(np.random.standard_normal((C, S))), "char_feat": f32(np.random.standard_normal((C, N))), "offs": striped(np.random.permutation(S)[:N])}


def reference(word_feat, char_feat, offs):
    idx = offs[:16].T.reshape(-1)
    return f64(word_feat)[:, idx] * RATE_HEAD + f64(char_feat) * (1.0 - RATE_HEAD)

@@ -1,0 +1,38 @@
+import concourse.mybir as mybir
+
+F32 = mybir.dt.float32
+U16 = mybir.dt.uint16
+ADD = mybir.AluOpType.add
+
+P = 128
+C, S, N = 512, 256, 128
+BLOCKS = C // P
+WORD_WEIGHT = 0.88
+CHAR_WEIGHT = 1.0 - WORD_WEIGHT
+
+
+def tile_slutagging_kernel(tc, word_feat, char_feat, offs, out):
+    nc = tc.nc
+    word_blocks = word_feat.rearrange("(b p) s -> b p s", p=P)
+    char_blocks = char_feat.rearrange("(b p) n -> b p n", p=P)
+    out_blocks = out.rearrange("(b p) n -> b p n", p=P)
+
+    with (
+        tc.tile_pool(name="held", bufs=1) as held,
+        tc.tile_pool(name="work", bufs=BLOCKS) as work,
+    ):
+        offsets = held.tile([P, N // 16], U16, name="offsets")
+        nc.sync.dma_start(offsets[:], offs)
+
+        for b in range(BLOCKS):
+            words = work.tile([P, S], F32, name="words")
+            chars = work.tile([P, N], F32, name="chars")
+            blend = work.tile([P, N], F32, name="blend")
+            nc.sync.dma_start(words[:], word_blocks[b])
+            nc.scalar.dma_start(chars[:], char_blocks[b])
+
+            nc.vector.tensor_scalar_mul(chars[:], chars[:], CHAR_WEIGHT / WORD_WEIGHT)
+            nc.vector.tensor_tensor(blend[:], words[:].indirect(offsets[:]), chars[:], ADD)
+            nc.vector.tensor_scalar_mul(blend[:], blend[:], WORD_WEIGHT)
+
+            nc.scalar.dma_start(out_blocks[b], blend[:])

@@ -31,8 +31,8 @@ def tile_slutagging_kernel(tc, word_feat, char_feat, offs, out):
             nc.sync.dma_start(words[:], word_blocks[b])
             nc.scalar.dma_start(chars[:], char_blocks[b])
 
-            nc.vector.tensor_scalar_mul(chars[:], chars[:], CHAR_WEIGHT / WORD_WEIGHT)
+            nc.scalar.mul(chars[:], chars[:], CHAR_WEIGHT / WORD_WEIGHT)
             nc.vector.tensor_tensor(blend[:], words[:].indirect(offsets[:]), chars[:], ADD)
             nc.vector.tensor_scalar_mul(blend[:], blend[:], WORD_WEIGHT)
 
-            nc.scalar.dma_start(out_blocks[b], blend[:])
+            nc.sync.dma_start(out_blocks[b], blend[:])

@@ -28,8 +28,8 @@ def tile_slutagging_kernel(tc, word_feat, char_feat, offs, out):
             words = work.tile([P, S], F32, name="words")
             chars = work.tile([P, N], F32, name="chars")
             blend = work.tile([P, N], F32, name="blend")
+            nc.sync.dma_start(chars[:], char_blocks[b])
             nc.sync.dma_start(words[:], word_blocks[b])
-            nc.scalar.dma_start(chars[:], char_blocks[b])
 
             nc.scalar.mul(chars[:], chars[:], CHAR_WEIGHT / WORD_WEIGHT)
             nc.vector.tensor_tensor(blend[:], words[:].indirect(offsets[:]), chars[:], ADD)

@@ -28,11 +28,11 @@ def tile_slutagging_kernel(tc, word_feat, char_feat, offs, out):
             words = work.tile([P, S], F32, name="words")
             chars = work.tile([P, N], F32, name="chars")
             blend = work.tile([P, N], F32, name="blend")
-            nc.sync.dma_start(chars[:], char_blocks[b])
             nc.sync.dma_start(words[:], word_blocks[b])
+            nc.scalar.dma_start(chars[:], char_blocks[b])
 
             nc.scalar.mul(chars[:], chars[:], CHAR_WEIGHT / WORD_WEIGHT)
             nc.vector.tensor_tensor(blend[:], words[:].indirect(offsets[:]), chars[:], ADD)
-            nc.vector.tensor_scalar_mul(blend[:], blend[:], WORD_WEIGHT)
+            nc.scalar.mul(blend[:], blend[:], WORD_WEIGHT)
 
             nc.sync.dma_start(out_blocks[b], blend[:])

@@ -11,11 +11,14 @@ WORD_WEIGHT = 0.88
 CHAR_WEIGHT = 1.0 - WORD_WEIGHT
 
 
+HALF = BLOCKS // 2
+
+
 def tile_slutagging_kernel(tc, word_feat, char_feat, offs, out):
     nc = tc.nc
-    word_blocks = word_feat.rearrange("(b p) s -> b p s", p=P)
-    char_blocks = char_feat.rearrange("(b p) n -> b p n", p=P)
-    out_blocks = out.rearrange("(b p) n -> b p n", p=P)
+    word_blocks = word_feat.rearrange("(p b) s -> b p s", b=BLOCKS)
+    char_halves = char_feat.rearrange("(p h b) n -> h p (b n)", h=2, b=HALF)
+    out_blocks = out.rearrange("(p b) n -> b p n", b=BLOCKS)
 
     with (
         tc.tile_pool(name="held", bufs=1) as held,
@@ -24,15 +27,18 @@ def tile_slutagging_kernel(tc, word_feat, char_feat, offs, out):
         offsets = held.tile([P, N // 16], U16, name="offsets")
         nc.sync.dma_start(offsets[:], offs)
 
-        for b in range(BLOCKS):
-            words = work.tile([P, S], F32, name="words")
-            chars = work.tile([P, N], F32, name="chars")
-            blend = work.tile([P, N], F32, name="blend")
-            nc.sync.dma_start(words[:], word_blocks[b])
-            nc.scalar.dma_start(chars[:], char_blocks[b])
-
+        for h in range(2):
+            chars = work.tile([P, HALF * N], F32, name="chars")
+            nc.scalar.dma_start(chars[:], char_halves[h])
             nc.scalar.mul(chars[:], chars[:], CHAR_WEIGHT / WORD_WEIGHT)
-            nc.vector.tensor_tensor(blend[:], words[:].indirect(offsets[:]), chars[:], ADD)
-            nc.scalar.mul(blend[:], blend[:], WORD_WEIGHT)
 
-            nc.sync.dma_start(out_blocks[b], blend[:])
+            for i in range(HALF):
+                b = h * HALF + i
+                words = work.tile([P, S], F32, name="words")
+                blend = work.tile([P, N], F32, name="blend")
+                nc.sync.dma_start(words[:], word_blocks[b])
+                nc.vector.tensor_tensor(
+                    blend[:], words[:].indirect(offsets[:]), chars[:, i * N : (i + 1) * N], ADD
+                )
+                nc.vector.tensor_scalar_mul(blend[:], blend[:], WORD_WEIGHT)
+                nc.sync.dma_start(out_blocks[b], blend[:])

@@ -40,5 +40,5 @@ def tile_slutagging_kernel(tc, word_feat, char_feat, offs, out):
                 nc.vector.tensor_tensor(
                     blend[:], words[:].indirect(offsets[:]), chars[:, i * N : (i + 1) * N], ADD
                 )
-                nc.vector.tensor_scalar_mul(blend[:], blend[:], WORD_WEIGHT)
+                nc.scalar.mul(blend[:], blend[:], WORD_WEIGHT)
                 nc.sync.dma_start(out_blocks[b], blend[:])

@@ -30,15 +30,16 @@ def tile_slutagging_kernel(tc, word_feat, char_feat, offs, out):
         for h in range(2):
             chars = work.tile([P, HALF * N], F32, name="chars")
             nc.scalar.dma_start(chars[:], char_halves[h])
-            nc.scalar.mul(chars[:], chars[:], CHAR_WEIGHT / WORD_WEIGHT)
 
             for i in range(HALF):
                 b = h * HALF + i
                 words = work.tile([P, S], F32, name="words")
                 blend = work.tile([P, N], F32, name="blend")
                 nc.sync.dma_start(words[:], word_blocks[b])
-                nc.vector.tensor_tensor(
-                    blend[:], words[:].indirect(offsets[:]), chars[:, i * N : (i + 1) * N], ADD
-                )
+
+                char_term = chars[:, i * N : (i + 1) * N]
+                nc.scalar.mul(char_term, char_term, CHAR_WEIGHT / WORD_WEIGHT)
+                nc.vector.tensor_tensor(blend[:], words[:].indirect(offsets[:]), char_term, ADD)
                 nc.scalar.mul(blend[:], blend[:], WORD_WEIGHT)
+
                 nc.sync.dma_start(out_blocks[b], blend[:])

@@ -40,6 +40,9 @@ def tile_slutagging_kernel(tc, word_feat, char_feat, offs, out):
                 char_term = chars[:, i * N : (i + 1) * N]
                 nc.scalar.mul(char_term, char_term, CHAR_WEIGHT / WORD_WEIGHT)
                 nc.vector.tensor_tensor(blend[:], words[:].indirect(offsets[:]), char_term, ADD)
-                nc.scalar.mul(blend[:], blend[:], WORD_WEIGHT)
+                if b < BLOCKS - 1:
+                    nc.scalar.mul(blend[:], blend[:], WORD_WEIGHT)
+                else:
+                    nc.vector.tensor_scalar_mul(blend[:], blend[:], WORD_WEIGHT)
 
                 nc.sync.dma_start(out_blocks[b], blend[:])

@@ -12,6 +12,7 @@ CHAR_WEIGHT = 1.0 - WORD_WEIGHT
 
 
 HALF = BLOCKS // 2
+AXI_BYTES = 256
 
 
 def tile_slutagging_kernel(tc, word_feat, char_feat, offs, out):
@@ -28,13 +29,13 @@ def tile_slutagging_kernel(tc, word_feat, char_feat, offs, out):
         nc.sync.dma_start(offsets[:], offs)
 
         for h in range(2):
-            chars = work.tile([P, HALF * N], F32, name="chars")
+            chars = work.tile([P, HALF * N], F32, name="chars", align_bytes=AXI_BYTES)
             nc.scalar.dma_start(chars[:], char_halves[h])
 
             for i in range(HALF):
                 b = h * HALF + i
-                words = work.tile([P, S], F32, name="words")
-                blend = work.tile([P, N], F32, name="blend")
+                words = work.tile([P, S], F32, name="words", align_bytes=AXI_BYTES)
+                blend = work.tile([P, N], F32, name="blend", align_bytes=AXI_BYTES)
                 nc.sync.dma_start(words[:], word_blocks[b])
 
                 char_term = chars[:, i * N : (i + 1) * N]

@@ -9,8 +9,6 @@ C, S, N = 512, 256, 128
 BLOCKS = C // P
 WORD_WEIGHT = 0.88
 CHAR_WEIGHT = 1.0 - WORD_WEIGHT
-
-
 HALF = BLOCKS // 2
 AXI_BYTES = 256
 
@@ -28,22 +26,24 @@ def tile_slutagging_kernel(tc, word_feat, char_feat, offs, out):
         offsets = held.tile([P, N // 16], U16, name="offsets")
         nc.sync.dma_start(offsets[:], offs)
 
+        chars = []
+        words = []
         for h in range(2):
-            chars = work.tile([P, HALF * N], F32, name="chars", align_bytes=AXI_BYTES)
-            nc.scalar.dma_start(chars[:], char_halves[h])
+            chars.append(work.tile([P, HALF * N], F32, name="chars", align_bytes=AXI_BYTES))
+            nc.scalar.dma_start(chars[h][:], char_halves[h])
+            for b in range(h * HALF, (h + 1) * HALF):
+                words.append(work.tile([P, S], F32, name="words", align_bytes=AXI_BYTES))
+                nc.sync.dma_start(words[b][:], word_blocks[b])
 
-            for i in range(HALF):
-                b = h * HALF + i
-                words = work.tile([P, S], F32, name="words", align_bytes=AXI_BYTES)
-                blend = work.tile([P, N], F32, name="blend", align_bytes=AXI_BYTES)
-                nc.sync.dma_start(words[:], word_blocks[b])
+        for h in range(2):
+            nc.scalar.mul(chars[h][:], chars[h][:], CHAR_WEIGHT / WORD_WEIGHT)
 
-                char_term = chars[:, i * N : (i + 1) * N]
-                nc.scalar.mul(char_term, char_term, CHAR_WEIGHT / WORD_WEIGHT)
-                nc.vector.tensor_tensor(blend[:], words[:].indirect(offsets[:]), char_term, ADD)
-                if b < BLOCKS - 1:
-                    nc.scalar.mul(blend[:], blend[:], WORD_WEIGHT)
-                else:
-                    nc.vector.tensor_scalar_mul(blend[:], blend[:], WORD_WEIGHT)
-
-                nc.sync.dma_start(out_blocks[b], blend[:])
+        for b in range(BLOCKS):
+            char_term = chars[b // HALF][:, (b % HALF) * N : (b % HALF + 1) * N]
+            blend = work.tile([P, N], F32, name="blend", align_bytes=AXI_BYTES)
+            nc.vector.tensor_tensor(blend[:], words[b][:].indirect(offsets[:]), char_term, ADD)
+            if b < BLOCKS - 1:
+                nc.scalar.mul(blend[:], blend[:], WORD_WEIGHT)
+            else:
+                nc.vector.tensor_scalar_mul(blend[:], blend[:], WORD_WEIGHT)
+            nc.sync.dma_start(out_blocks[b], blend[:])

@@ -15,9 +15,9 @@ AXI_BYTES = 256
 
 def tile_slutagging_kernel(tc, word_feat, char_feat, offs, out):
     nc = tc.nc
-    word_blocks = word_feat.rearrange("(p b) s -> b p s", b=BLOCKS)
-    char_halves = char_feat.rearrange("(p h b) n -> h p (b n)", h=2, b=HALF)
-    out_blocks = out.rearrange("(p b) n -> b p n", b=BLOCKS)
+    word_blocks = word_feat.rearrange("(h p b) s -> h b p s", h=2, b=HALF)
+    char_halves = char_feat.rearrange("(h p b) n -> h p (b n)", h=2, b=HALF)
+    out_blocks = out.rearrange("(h p b) n -> h b p n", h=2, b=HALF)
 
     with (
         tc.tile_pool(name="held", bufs=1) as held,
@@ -33,7 +33,7 @@ def tile_slutagging_kernel(tc, word_feat, char_feat, offs, out):
             nc.scalar.dma_start(chars[h][:], char_halves[h])
             for b in range(h * HALF, (h + 1) * HALF):
                 words.append(work.tile([P, S], F32, name="words", align_bytes=AXI_BYTES))
-                nc.sync.dma_start(words[b][:], word_blocks[b])
+                nc.sync.dma_start(words[b][:], word_blocks[h, b % HALF])
 
         for h in range(2):
             nc.scalar.mul(chars[h][:], chars[h][:], CHAR_WEIGHT / WORD_WEIGHT)
@@ -46,4 +46,4 @@ def tile_slutagging_kernel(tc, word_feat, char_feat, offs, out):
                 nc.scalar.mul(blend[:], blend[:], WORD_WEIGHT)
             else:
                 nc.vector.tensor_scalar_mul(blend[:], blend[:], WORD_WEIGHT)
-            nc.sync.dma_start(out_blocks[b], blend[:])
+            nc.sync.dma_start(out_blocks[b // HALF, b % HALF], blend[:])

@@ -33,7 +33,8 @@ def tile_slutagging_kernel(tc, word_feat, char_feat, offs, out):
             nc.scalar.dma_start(chars[h][:], char_halves[h])
             for b in range(h * HALF, (h + 1) * HALF):
                 words.append(work.tile([P, S], F32, name="words", align_bytes=AXI_BYTES))
-                nc.sync.dma_start(words[b][:], word_blocks[h, b % HALF])
+                queue = nc.scalar if b == BLOCKS - 2 else nc.sync
+                queue.dma_start(words[b][:], word_blocks[h, b % HALF])
 
         for h in range(2):
             nc.scalar.mul(chars[h][:], chars[h][:], CHAR_WEIGHT / WORD_WEIGHT)

import concourse.mybir as mybir

F32 = mybir.dt.float32
U16 = mybir.dt.uint16
ADD = mybir.AluOpType.add

P = 128
C, S, N = 512, 256, 128
BLOCKS = C // P
WORD_WEIGHT = 0.88
CHAR_WEIGHT = 1.0 - WORD_WEIGHT
HALF = BLOCKS // 2
AXI_BYTES = 256


def tile_slutagging_kernel(tc, word_feat, char_feat, offs, out):
    nc = tc.nc
    word_blocks = word_feat.rearrange("(h p b) s -> h b p s", h=2, b=HALF)
    char_halves = char_feat.rearrange("(h p b) n -> h p (b n)", h=2, b=HALF)
    out_blocks = out.rearrange("(h p b) n -> h b p n", h=2, b=HALF)

    with (
        tc.tile_pool(name="held", bufs=1) as held,
        tc.tile_pool(name="work", bufs=BLOCKS) as work,
    ):
        offsets = held.tile([P, N // 16], U16, name="offsets")
        nc.sync.dma_start(offsets[:], offs)

        chars = []
        words = []
        for h in range(2):
            chars.append(work.tile([P, HALF * N], F32, name="chars", align_bytes=AXI_BYTES))
            nc.scalar.dma_start(chars[h][:], char_halves[h])
            for b in range(h * HALF, (h + 1) * HALF):
                words.append(work.tile([P, S], F32, name="words", align_bytes=AXI_BYTES))
                queue = nc.scalar if b == BLOCKS - 2 else nc.sync
                queue.dma_start(words[b][:], word_blocks[h, b % HALF])

        for h in range(2):
            nc.scalar.mul(chars[h][:], chars[h][:], CHAR_WEIGHT / WORD_WEIGHT)

        for b in range(BLOCKS):
            char_term = chars[b // HALF][:, (b % HALF) * N : (b % HALF + 1) * N]
            blend = work.tile([P, N], F32, name="blend", align_bytes=AXI_BYTES)
            nc.vector.tensor_tensor(blend[:], words[b][:].indirect(offsets[:]), char_term, ADD)
            if b < BLOCKS - 1:
                nc.scalar.mul(blend[:], blend[:], WORD_WEIGHT)
            else:
                nc.vector.tensor_scalar_mul(blend[:], blend[:], WORD_WEIGHT)
            nc.sync.dma_start(out_blocks[b // HALF, b % HALF], blend[:])
